import numpy as np
import ml_dtypes


def mxq(x, axis, fmt="e4m3"):
    dtype, down = {"e4m3": (ml_dtypes.float8_e4m3fn, 7), "e5m2": (ml_dtypes.float8_e5m2, 14)}[fmt]
    v = np.moveaxis(np.asarray(x, np.float32).astype(ml_dtypes.bfloat16).astype(np.float64), axis, -1)
    blocks = v.reshape(v.shape[:-1] + (-1, 32))
    amax = np.abs(blocks).max(-1, keepdims=True)
    byte = np.maximum(np.where(amax > 0, np.frexp(amax)[1] - 1 + 127, 0) - down, 1)
    scale = np.exp2(byte - 127.0)
    codes = (blocks / scale).astype(np.float32).astype(dtype).astype(np.float64)
    return np.moveaxis((codes * scale).reshape(v.shape), -1, axis)


WIDE = False


def mx_kscale(k):
    if not WIDE:
        return np.ones(k)
    levels = np.array([10, -10, 5, -5, 0])
    if k % 512:
        return np.exp2(np.random.permutation(np.resize(levels, k // 32))).repeat(32)
    a = np.empty((k // 512, 16))
    for p in range(k // 512):
        a[p, :8] = np.random.permutation(np.resize(levels, 8))
        for g in range(8):
            far = levels[np.abs(levels - a[p, g]) >= 10]
            a[p, g + 8] = far[np.random.randint(len(far))]
    return np.exp2(a.ravel()).repeat(32)


BF16 = ml_dtypes.bfloat16


def bf(x):
    return np.asarray(x, np.float32).astype(BF16)


def f64(x):
    return np.asarray(x).astype(np.float64)


B, S, D, H, HD, P = 4, 256, 512, 2, 128, 512
N = H * HD
THETA = 500000.0


def rope(t, cos, sin):
    tr = t[..., 0::2]
    ti = t[..., 1::2]
    c = cos[None, :, None, :]
    s = sin[None, :, None, :]
    out = np.stack([tr * c - ti * s, tr * s + ti * c], axis=-1)
    return out.reshape(t.shape)


def setup_inputs():
    s = mx_kscale(D)
    inv = 1.0 / THETA ** (np.arange(0, HD, 2) / HD)
    ang = np.outer(np.arange(S), inv)
    return {"x": bf(np.random.standard_normal((B, S, D)) * s),
            "wq": bf(np.random.standard_normal((N, D)) / np.sqrt(D) / s[None, :]),
            "wk": bf(np.random.standard_normal((N, D)) / np.sqrt(D) / s[None, :]),
            "freqs_cos": bf(np.cos(ang)),
            "freqs_sin": bf(np.sin(ang))}


def reference(x, wq, wk, freqs_cos, freqs_sin):
    xm = mxq(f64(x), 2, "e4m3")
    xq = (xm @ mxq(f64(wq), 1, "e4m3").T).reshape(B, S, H, HD)
    xk = (xm @ mxq(f64(wk), 1, "e4m3").T).reshape(B, S, H, HD)
    q = rope(xq, f64(freqs_cos), f64(freqs_sin)).transpose(0, 2, 1, 3)
    k = rope(xk, f64(freqs_cos), f64(freqs_sin)).transpose(0, 2, 1, 3)
    return q, k

@@ -1,0 +1,164 @@
+import concourse.mybir as mybir
+from concourse.masks import make_identity
+
+BF16 = mybir.dt.bfloat16
+F32 = mybir.dt.float32
+U32 = mybir.dt.uint32
+U8 = mybir.dt.uint8
+FP8X4 = mybir.dt.float8_e4m3fn_x4
+MULT = mybir.AluOpType.mult
+ADD = mybir.AluOpType.add
+SUBTRACT = mybir.AluOpType.subtract
+
+P = 128
+BATCH = 4
+SEQ = 256
+K = 512
+PACK = 4
+HALVES = 2
+HEADS = 2
+HEAD_DIM = 128
+FREQS = HEAD_DIM // 2
+POS = SEQ // P
+PAIR = 2
+MATS = 2
+GROUPS = MATS * HEADS
+TERM_MEMBERS = ((0,), (1,), (0, 1))
+TERMS = len(TERM_MEMBERS)
+GPSIMD_SUMS = 4
+PSUM_BANKS = 8
+
+FLOPS = 2 * BATCH * SEQ * K * MATS * HEADS * HEAD_DIM
+
+
+def tile_attention_pa_s_kernel(tc, x, wq, wk, freqs_cos, freqs_sin, out_0, out_1):
+    nc = tc.nc
+    with (
+        tc.tile_pool(name="keep", bufs=1) as keep,
+        tc.tile_pool(name="work", bufs=BATCH) as work,
+        tc.psum_pool(name="banks", bufs=PSUM_BANKS) as banks,
+        tc.manual_schedule(),
+    ):
+        w_rows = keep.tile([P, MATS, PAIR, K], BF16)
+        nc.sync.dma_start(out=w_rows[:, 0], in_=wq.rearrange("(n e) k -> n e k", e=PAIR))
+        nc.sync.dma_start(out=w_rows[:, 1], in_=wk.rearrange("(n e) k -> n e k", e=PAIR))
+        x_rows = keep.tile([P, BATCH, POS, K], BF16)
+        for b in range(BATCH):
+            nc.sync.dma_start(out=x_rows[:, b], in_=x[b].rearrange("(p t) k -> p t k", t=POS))
+        cos = keep.tile([P, POS, FREQS], BF16)
+        sin = keep.tile([P, POS, FREQS], BF16)
+        nc.scalar.dma_start(out=cos[:], in_=freqs_cos.rearrange("(p t) i -> p t i", t=POS))
+        nc.scalar.dma_start(out=sin[:], in_=freqs_sin.rearrange("(p t) i -> p t i", t=POS))
+
+        identity = keep.tile([P, P], F32)
+        make_identity(nc, identity[:])
+        minus_cos = keep.tile([P, POS, FREQS], F32)
+        minus_cos_minus_sin = keep.tile([P, POS, FREQS], F32)
+        sin_minus_cos = keep.tile([P, POS, FREQS], F32)
+        nc.gpsimd.tensor_scalar(
+            out=minus_cos[:], in0=cos[:], scalar1=-1.0, scalar2=0.0, op0=MULT, op1=ADD
+        )
+        nc.gpsimd.tensor_tensor(out=minus_cos_minus_sin[:], in0=minus_cos[:], in1=sin[:], op=SUBTRACT)
+        nc.gpsimd.tensor_tensor(out=sin_minus_cos[:], in0=sin[:], in1=cos[:], op=SUBTRACT)
+        term_factors = (sin_minus_cos, minus_cos_minus_sin, cos)
+
+        def transpose_and_group(rows, grouped, copy):
+            flipped = banks.tile([P, 2, HALVES, P], F32, tag="bank")
+            for s in range(2):
+                words = rows[:, s, :].bitcast(F32)
+                for u in range(HALVES):
+                    nc.tensor.transpose(
+                        flipped[:, s, u, :], words[:, u::HALVES], identity[:]
+                    )
+            copy(out=grouped, in_=flipped[:].rearrange("p s u r -> p s r u"))
+
+        w_grouped = keep.tile([P, PAIR, MATS, P, PACK], BF16, align_bytes=64)
+        w_grouped_words = w_grouped[:].bitcast(F32)
+        transpose_and_group(w_rows[:, 0], w_grouped_words[:, :, 0], nc.scalar.copy)
+        transpose_and_group(w_rows[:, 1], w_grouped_words[:, :, 1], nc.vector.tensor_copy)
+        x_grouped = keep.tile([P, BATCH, POS, P, PACK], BF16, align_bytes=64)
+        for b in range(BATCH):
+            transpose_and_group(x_rows[:, b], x_grouped[:, b].bitcast(F32), nc.scalar.copy)
+
+        w_codes = keep.tile([P, PAIR, MATS * P], U32, align_bytes=64)
+        w_scales = keep.tile([P, PAIR, MATS * P], U8, align_bytes=64)
+        x_codes = keep.tile([P, BATCH, POS * P], U32, align_bytes=64)
+        x_scales = keep.tile([P, BATCH, POS * P], U8, align_bytes=64)
+
+        def quantise_x(b):
+            nc.vector.quantize_mx(
+                out=x_codes[:, b, :].bitcast(FP8X4),
+                scales=x_scales[:, b, :],
+                in_=x_grouped[:, b].rearrange("p t r j -> p (t r j)"),
+            )
+
+        def project(b):
+            projected = []
+            for j, members in enumerate(TERM_MEMBERS):
+                bank = banks.tile([P, POS, GROUPS, FREQS], F32, tag="bank", name="projected%d" % j)
+                for t in range(POS):
+                    for e in members:
+                        nc.tensor.matmul_mx(
+                            out=bank[:, t].rearrange("p g i -> p (g i)"),
+                            lhsT=x_codes[:, b, t * P : (t + 1) * P].bitcast(FP8X4),
+                            lhsT_scale=x_scales[:, b, t * P : (t + 1) * P],
+                            rhs=w_codes[:, e, :].bitcast(FP8X4),
+                            rhs_scale=w_scales[:, e, :],
+                            start=(e == members[0]),
+                            stop=(e == members[-1]),
+                        )
+                projected.append(bank)
+            return projected
+
+        def new_terms():
+            own = work.tile([P, PAIR, POS, GROUPS, FREQS], F32)
+            shared = work.tile([P, POS, GROUPS, FREQS], F32)
+            return own, shared
+
+        def form_term(j, projected, own, shared):
+            nc.vector.tensor_tensor(
+                out=(own[:, 1], own[:, 0], shared[:])[j],
+                in0=projected[j][:],
+                in1=term_factors[j][:].unsqueeze(2).to_broadcast([P, POS, GROUPS, FREQS]),
+                op=MULT,
+            )
+
+        def sum_and_store(b, own, shared):
+            rotated = work.tile([P, GROUPS, POS, FREQS, PAIR], F32)
+            for m, result in enumerate((out_0, out_1)):
+                heads = slice(m * HEADS, (m + 1) * HEADS)
+                if MATS * b + m < GPSIMD_SUMS:
+                    adder, store_queue = nc.gpsimd, nc.scalar
+                else:
+                    adder, store_queue = nc.vector, nc.sync
+                adder.tensor_tensor(
+                    out=rotated[:, heads].rearrange("p h t i e -> p t h i e"),
+                    in0=shared[:, :, heads].unsqueeze(4).to_broadcast([P, POS, HEADS, FREQS, PAIR]),
+                    in1=own[:, :, :, heads].rearrange("p e t h i -> p t h i e"),
+                    op=ADD,
+                )
+                store_queue.dma_start(
+                    out=result[b].rearrange("h (p t) d -> p h (t d)", t=POS),
+                    in_=rotated[:, heads].rearrange("p h t i e -> p h (t i e)"),
+                )
+
+        nc.vector.quantize_mx(
+            out=w_codes[:].rearrange("p e c -> p (e c)").bitcast(FP8X4),
+            scales=w_scales[:].rearrange("p e c -> p (e c)"),
+            in_=w_grouped[:].rearrange("p e m n j -> p (e m n j)"),
+        )
+        quantise_x(0)
+        projected = project(0)
+        own, shared = new_terms()
+        assert BATCH - 1 == TERMS
+        for j in range(TERMS):
+            quantise_x(j + 1)
+            form_term(j, projected, own, shared)
+        sum_and_store(0, own, shared)
+
+        for b in range(1, BATCH):
+            projected = project(b)
+            own, shared = new_terms()
+            for j in range(TERMS):
+                form_term(j, projected, own, shared)
+            sum_and_store(b, own, shared)

@@ -21,11 +21,11 @@ HEAD_DIM = 128
 FREQS = HEAD_DIM // 2
 POS = SEQ // P
 PAIR = 2
+EVEN, ODD = 0, 1
 MATS = 2
-GROUPS = MATS * HEADS
-TERM_MEMBERS = ((0,), (1,), (0, 1))
-TERMS = len(TERM_MEMBERS)
-GPSIMD_SUMS = 4
+WQ, WK = 0, 1
+UNITS = BATCH * MATS
+GPSIMD_UNITS = 5
 PSUM_BANKS = 8
 
 FLOPS = 2 * BATCH * SEQ * K * MATS * HEADS * HEAD_DIM
@@ -35,16 +35,24 @@ def tile_attention_pa_s_kernel(tc, x, wq, wk, freqs_cos, freqs_sin, out_0, out_1
     nc = tc.nc
     with (
         tc.tile_pool(name="keep", bufs=1) as keep,
-        tc.tile_pool(name="work", bufs=BATCH) as work,
+        tc.tile_pool(name="work", bufs=UNITS) as work,
         tc.psum_pool(name="banks", bufs=PSUM_BANKS) as banks,
         tc.manual_schedule(),
     ):
         w_rows = keep.tile([P, MATS, PAIR, K], BF16)
-        nc.sync.dma_start(out=w_rows[:, 0], in_=wq.rearrange("(n e) k -> n e k", e=PAIR))
-        nc.sync.dma_start(out=w_rows[:, 1], in_=wk.rearrange("(n e) k -> n e k", e=PAIR))
         x_rows = keep.tile([P, BATCH, POS, K], BF16)
-        for b in range(BATCH):
+
+        def load_w(m, w):
+            nc.sync.dma_start(out=w_rows[:, m], in_=w.rearrange("(n e) k -> n e k", e=PAIR))
+
+        def load_x(b):
             nc.sync.dma_start(out=x_rows[:, b], in_=x[b].rearrange("(p t) k -> p t k", t=POS))
+
+        load_w(WQ, wq)
+        load_x(0)
+        load_w(WK, wk)
+        for b in range(1, BATCH):
+            load_x(b)
         cos = keep.tile([P, POS, FREQS], BF16)
         sin = keep.tile([P, POS, FREQS], BF16)
         nc.scalar.dma_start(out=cos[:], in_=freqs_cos.rearrange("(p t) i -> p t i", t=POS))
@@ -53,112 +61,159 @@ def tile_attention_pa_s_kernel(tc, x, wq, wk, freqs_cos, freqs_sin, out_0, out_1
         identity = keep.tile([P, P], F32)
         make_identity(nc, identity[:])
         minus_cos = keep.tile([P, POS, FREQS], F32)
-        minus_cos_minus_sin = keep.tile([P, POS, FREQS], F32)
-        sin_minus_cos = keep.tile([P, POS, FREQS], F32)
+        own_factors = keep.tile([P, PAIR, POS, FREQS], F32)
         nc.gpsimd.tensor_scalar(
             out=minus_cos[:], in0=cos[:], scalar1=-1.0, scalar2=0.0, op0=MULT, op1=ADD
         )
-        nc.gpsimd.tensor_tensor(out=minus_cos_minus_sin[:], in0=minus_cos[:], in1=sin[:], op=SUBTRACT)
-        nc.gpsimd.tensor_tensor(out=sin_minus_cos[:], in0=sin[:], in1=cos[:], op=SUBTRACT)
-        term_factors = (sin_minus_cos, minus_cos_minus_sin, cos)
+        nc.gpsimd.tensor_tensor(out=own_factors[:, EVEN], in0=minus_cos[:], in1=sin[:], op=SUBTRACT)
+        nc.gpsimd.tensor_tensor(out=own_factors[:, ODD], in0=sin[:], in1=cos[:], op=SUBTRACT)
 
-        def transpose_and_group(rows, grouped, copy):
-            flipped = banks.tile([P, 2, HALVES, P], F32, tag="bank")
-            for s in range(2):
+        def transpose(rows):
+            sets = rows.shape[1]
+            flipped = banks.tile([P, sets, HALVES, P], F32, tag="bank")
+            for s in range(sets):
                 words = rows[:, s, :].bitcast(F32)
                 for u in range(HALVES):
-                    nc.tensor.transpose(
-                        flipped[:, s, u, :], words[:, u::HALVES], identity[:]
-                    )
-            copy(out=grouped, in_=flipped[:].rearrange("p s u r -> p s r u"))
+                    nc.tensor.transpose(flipped[:, s, u, :], words[:, u::HALVES], identity[:])
+            return flipped
 
-        w_grouped = keep.tile([P, PAIR, MATS, P, PACK], BF16, align_bytes=64)
-        w_grouped_words = w_grouped[:].bitcast(F32)
-        transpose_and_group(w_rows[:, 0], w_grouped_words[:, :, 0], nc.scalar.copy)
-        transpose_and_group(w_rows[:, 1], w_grouped_words[:, :, 1], nc.vector.tensor_copy)
+        def group(copy, grouped, flipped):
+            copy(out=grouped.bitcast(F32), in_=flipped[:].rearrange("p s u r -> p s r u"))
+
+        w_grouped = keep.tile([P, MATS, PAIR, P, PACK], BF16, align_bytes=64)
         x_grouped = keep.tile([P, BATCH, POS, P, PACK], BF16, align_bytes=64)
-        for b in range(BATCH):
-            transpose_and_group(x_rows[:, b], x_grouped[:, b].bitcast(F32), nc.scalar.copy)
-
-        w_codes = keep.tile([P, PAIR, MATS * P], U32, align_bytes=64)
-        w_scales = keep.tile([P, PAIR, MATS * P], U8, align_bytes=64)
+        w_codes = keep.tile([P, MATS, PAIR * P], U32, align_bytes=64)
+        w_scales = keep.tile([P, MATS, PAIR * P], U8, align_bytes=64)
         x_codes = keep.tile([P, BATCH, POS * P], U32, align_bytes=64)
         x_scales = keep.tile([P, BATCH, POS * P], U8, align_bytes=64)
 
-        def quantise_x(b):
+        def quantise_w(m):
             nc.vector.quantize_mx(
-                out=x_codes[:, b, :].bitcast(FP8X4),
-                scales=x_scales[:, b, :],
-                in_=x_grouped[:, b].rearrange("p t r j -> p (t r j)"),
+                out=w_codes[:, m].bitcast(FP8X4),
+                scales=w_scales[:, m],
+                in_=w_grouped[:, m].rearrange("p e n j -> p (e n j)"),
             )
 
-        def project(b):
-            projected = []
-            for j, members in enumerate(TERM_MEMBERS):
-                bank = banks.tile([P, POS, GROUPS, FREQS], F32, tag="bank", name="projected%d" % j)
-                for t in range(POS):
-                    for e in members:
-                        nc.tensor.matmul_mx(
-                            out=bank[:, t].rearrange("p g i -> p (g i)"),
-                            lhsT=x_codes[:, b, t * P : (t + 1) * P].bitcast(FP8X4),
-                            lhsT_scale=x_scales[:, b, t * P : (t + 1) * P],
-                            rhs=w_codes[:, e, :].bitcast(FP8X4),
-                            rhs_scale=w_scales[:, e, :],
-                            start=(e == members[0]),
-                            stop=(e == members[-1]),
-                        )
-                projected.append(bank)
-            return projected
+        def quantise_x(first, count):
+            batches = slice(first, first + count)
+            nc.vector.quantize_mx(
+                out=x_codes[:, batches].rearrange("p b c -> p (b c)").bitcast(FP8X4),
+                scales=x_scales[:, batches].rearrange("p b c -> p (b c)"),
+                in_=x_grouped[:, batches].rearrange("p b t r j -> p (b t r j)"),
+            )
 
-        def new_terms():
-            own = work.tile([P, PAIR, POS, GROUPS, FREQS], F32)
-            shared = work.tile([P, POS, GROUPS, FREQS], F32)
-            return own, shared
+        def project(out, b, t, m, members):
+            for e in members:
+                nc.tensor.matmul_mx(
+                    out=out,
+                    lhsT=x_codes[:, b, t * P : (t + 1) * P].bitcast(FP8X4),
+                    lhsT_scale=x_scales[:, b, t * P : (t + 1) * P],
+                    rhs=w_codes[:, m, e * P : (e + 1) * P].bitcast(FP8X4),
+                    rhs_scale=w_scales[:, m, e * P : (e + 1) * P],
+                    start=(e == members[0]),
+                    stop=(e == members[-1]),
+                )
 
-        def form_term(j, projected, own, shared):
+        def project_members(b, m):
+            bank = banks.tile([P, PAIR, POS, HEADS, FREQS], F32, tag="bank", name="members")
+            for t in range(POS):
+                for e in range(PAIR):
+                    project(bank[:, e, t].rearrange("p h i -> p (h i)"), b, t, m, (1 - e,))
+            return bank
+
+        def project_sums(b):
+            bank = banks.tile([P, POS, MATS * HEADS, FREQS], F32, tag="bank", name="sums")
+            for t in range(POS):
+                for m in range(MATS):
+                    groups = slice(m * HEADS, (m + 1) * HEADS)
+                    project(bank[:, t, groups].rearrange("p h i -> p (h i)"), b, t, m, (EVEN, ODD))
+            return bank
+
+        def form_own(bank):
+            own = work.tile([P, PAIR, POS, HEADS, FREQS], F32, name="own")
             nc.vector.tensor_tensor(
-                out=(own[:, 1], own[:, 0], shared[:])[j],
-                in0=projected[j][:],
-                in1=term_factors[j][:].unsqueeze(2).to_broadcast([P, POS, GROUPS, FREQS]),
+                out=own[:].rearrange("p e t h i -> p (e t) h i"),
+                in0=bank[:].rearrange("p e t h i -> p (e t) h i"),
+                in1=own_factors[:]
+                .rearrange("p e t i -> p (e t) i")
+                .unsqueeze(2)
+                .to_broadcast([P, PAIR * POS, HEADS, FREQS]),
                 op=MULT,
             )
+            return own
 
-        def sum_and_store(b, own, shared):
-            rotated = work.tile([P, GROUPS, POS, FREQS, PAIR], F32)
-            for m, result in enumerate((out_0, out_1)):
-                heads = slice(m * HEADS, (m + 1) * HEADS)
-                if MATS * b + m < GPSIMD_SUMS:
-                    adder, store_queue = nc.gpsimd, nc.scalar
-                else:
-                    adder, store_queue = nc.vector, nc.sync
+        def form_shared(bank):
+            shared = work.tile([P, POS, MATS * HEADS, FREQS], F32, name="shared")
+            nc.vector.tensor_tensor(
+                out=shared[:],
+                in0=bank[:],
+                in1=cos[:].unsqueeze(2).to_broadcast([P, POS, MATS * HEADS, FREQS]),
+                op=MULT,
+            )
+            return shared
+
+        results = (out_0, out_1)
+
+        def add_and_store(adder, store_queue, b, m, own, shared, pieces):
+            rotated = work.tile([P, HEADS, POS, FREQS, PAIR], F32, name="rotated")
+            count = HEADS // pieces
+            for first in range(0, HEADS, count):
+                heads = slice(first, first + count)
+                groups = slice(m * HEADS + first, m * HEADS + first + count)
                 adder.tensor_tensor(
                     out=rotated[:, heads].rearrange("p h t i e -> p t h i e"),
-                    in0=shared[:, :, heads].unsqueeze(4).to_broadcast([P, POS, HEADS, FREQS, PAIR]),
+                    in0=shared[:, :, groups].unsqueeze(4).to_broadcast([P, POS, count, FREQS, PAIR]),
                     in1=own[:, :, :, heads].rearrange("p e t h i -> p t h i e"),
                     op=ADD,
                 )
                 store_queue.dma_start(
-                    out=result[b].rearrange("h (p t) d -> p h (t d)", t=POS),
+                    out=results[m][b, heads].rearrange("h (p t) d -> p h (t d)", t=POS),
                     in_=rotated[:, heads].rearrange("p h t i e -> p h (t i e)"),
                 )
 
-        nc.vector.quantize_mx(
-            out=w_codes[:].rearrange("p e c -> p (e c)").bitcast(FP8X4),
-            scales=w_scales[:].rearrange("p e c -> p (e c)"),
-            in_=w_grouped[:].rearrange("p e m n j -> p (e m n j)"),
-        )
-        quantise_x(0)
-        projected = project(0)
-        own, shared = new_terms()
-        assert BATCH - 1 == TERMS
-        for j in range(TERMS):
-            quantise_x(j + 1)
-            form_term(j, projected, own, shared)
-        sum_and_store(0, own, shared)
+        first_copies = (nc.vector.tensor_copy, nc.scalar.copy)
+        for rows, grouped in (
+            (w_rows[:, WQ], w_grouped[:, WQ]),
+            (x_rows[:, 0], x_grouped[:, 0]),
+        ):
+            for s, copy in enumerate(first_copies):
+                flipped = transpose(rows[:, s : s + 1])
+                group(copy, grouped[:, s : s + 1], flipped)
+        quantise_w(WQ)
+        flipped = transpose(w_rows[:, WK])
+        group(nc.scalar.copy, w_grouped[:, WK], flipped)
+        quantise_x(0, 1)
+        flipped = transpose(x_rows[:, 1])
+        group(nc.scalar.copy, x_grouped[:, 1], flipped)
+        members = {(0, WQ): project_members(0, WQ)}
+        quantise_w(WK)
+        flipped = transpose(x_rows[:, 2])
+        group(nc.scalar.copy, x_grouped[:, 2], flipped)
+        own = {(0, WQ): form_own(members[0, WQ])}
+        members[0, WK] = project_members(0, WK)
+        flipped = transpose(x_rows[:, 3])
+        group(nc.scalar.copy, x_grouped[:, 3], flipped)
+        sums = project_sums(0)
+        quantise_x(1, 1)
+        own[0, WK] = form_own(members[0, WK])
+        quantise_x(2, 1)
+        quantise_x(3, 1)
+        shared = form_shared(sums)
 
-        for b in range(1, BATCH):
-            projected = project(b)
-            own, shared = new_terms()
-            for j in range(TERMS):
-                form_term(j, projected, own, shared)
-            sum_and_store(b, own, shared)
+        late = []
+        for b in range(BATCH):
+            if b > 0:
+                members[b, WQ] = project_members(b, WQ)
+                sums = project_sums(b)
+                members[b, WK] = project_members(b, WK)
+                own[b, WQ] = form_own(members[b, WQ])
+                shared = form_shared(sums)
+                own[b, WK] = form_own(members[b, WK])
+            for m in range(MATS):
+                if MATS * b + m < GPSIMD_UNITS:
+                    add_and_store(nc.gpsimd, nc.scalar, b, m, own[b, m], shared, 1)
+                else:
+                    late.append((b, m, own[b, m], shared))
+        for b, m, own_term, shared_term in late:
+            last = (b, m) == (BATCH - 1, MATS - 1)
+            add_and_store(nc.vector, nc.sync, b, m, own_term, shared_term, 2 if last else 1)

@@ -25,7 +25,7 @@ EVEN, ODD = 0, 1
 MATS = 2
 WQ, WK = 0, 1
 UNITS = BATCH * MATS
-GPSIMD_UNITS = 5
+GPSIMD_UNITS = 3
 PSUM_BANKS = 8
 
 FLOPS = 2 * BATCH * SEQ * K * MATS * HEADS * HEAD_DIM

@@ -25,8 +25,8 @@ EVEN, ODD = 0, 1
 MATS = 2
 WQ, WK = 0, 1
 UNITS = BATCH * MATS
-GPSIMD_UNITS = 3
 PSUM_BANKS = 8
+WARM_UP = 4
 
 FLOPS = 2 * BATCH * SEQ * K * MATS * HEADS * HEAD_DIM
 
@@ -58,15 +58,21 @@ def tile_attention_pa_s_kernel(tc, x, wq, wk, freqs_cos, freqs_sin, out_0, out_1
         nc.scalar.dma_start(out=cos[:], in_=freqs_cos.rearrange("(p t) i -> p t i", t=POS))
         nc.scalar.dma_start(out=sin[:], in_=freqs_sin.rearrange("(p t) i -> p t i", t=POS))
 
+        ones = keep.tile([P, P], F32)
+        nc.vector.memset(ones[:], 1.0)
+        warm = banks.tile([P, WARM_UP, P], F32, tag="bank")
+        for j in range(WARM_UP):
+            nc.tensor.matmul(warm[:, j, :], ones[:], ones[:], start=True, stop=True)
+
         identity = keep.tile([P, P], F32)
         make_identity(nc, identity[:])
         minus_cos = keep.tile([P, POS, FREQS], F32)
-        own_factors = keep.tile([P, PAIR, POS, FREQS], F32)
+        own_factors = keep.tile([P, POS, FREQS, PAIR], F32)
         nc.gpsimd.tensor_scalar(
             out=minus_cos[:], in0=cos[:], scalar1=-1.0, scalar2=0.0, op0=MULT, op1=ADD
         )
-        nc.gpsimd.tensor_tensor(out=own_factors[:, EVEN], in0=minus_cos[:], in1=sin[:], op=SUBTRACT)
-        nc.gpsimd.tensor_tensor(out=own_factors[:, ODD], in0=sin[:], in1=cos[:], op=SUBTRACT)
+        nc.gpsimd.tensor_tensor(out=own_factors[:, :, :, EVEN], in0=minus_cos[:], in1=sin[:], op=SUBTRACT)
+        nc.gpsimd.tensor_tensor(out=own_factors[:, :, :, ODD], in0=sin[:], in1=cos[:], op=SUBTRACT)
 
         def transpose(rows):
             sets = rows.shape[1]
@@ -130,46 +136,64 @@ def tile_attention_pa_s_kernel(tc, x, wq, wk, freqs_cos, freqs_sin, out_0, out_1
             return bank
 
         def form_own(bank):
-            own = work.tile([P, PAIR, POS, HEADS, FREQS], F32, name="own")
+            own = work.tile([P, POS, HEADS, FREQS, PAIR], F32, name="own")
             nc.vector.tensor_tensor(
-                out=own[:].rearrange("p e t h i -> p (e t) h i"),
-                in0=bank[:].rearrange("p e t h i -> p (e t) h i"),
-                in1=own_factors[:]
-                .rearrange("p e t i -> p (e t) i")
-                .unsqueeze(2)
-                .to_broadcast([P, PAIR * POS, HEADS, FREQS]),
+                out=own[:],
+                in0=bank[:].rearrange("p e t h i -> p t h i e"),
+                in1=own_factors[:].unsqueeze(2).to_broadcast([P, POS, HEADS, FREQS, PAIR]),
                 op=MULT,
             )
             return own
 
         def form_shared(bank):
-            shared = work.tile([P, POS, MATS * HEADS, FREQS], F32, name="shared")
+            groups = MATS * HEADS
+            shared = work.tile([P, POS, groups, FREQS], F32, name="shared")
             nc.vector.tensor_tensor(
                 out=shared[:],
                 in0=bank[:],
-                in1=cos[:].unsqueeze(2).to_broadcast([P, POS, MATS * HEADS, FREQS]),
+                in1=cos[:].unsqueeze(2).to_broadcast([P, POS, groups, FREQS]),
                 op=MULT,
             )
-            return shared
+            return [shared[:, :, g : g + HEADS] for g in range(0, groups, HEADS)]
 
         results = (out_0, out_1)
 
-        def add_and_store(adder, store_queue, b, m, own, shared, pieces):
+        def span(heads):
+            return slice(heads[0], heads[-1] + 1)
+
+        def store(queue, unit, heads, rotated):
+            b, m = unit
+            queue.dma_start(
+                out=results[m][b, span(heads)].rearrange("h (p t) d -> p h (t d)", t=POS),
+                in_=rotated[:, span(heads)].rearrange("p h t i e -> p h (t i e)"),
+            )
+
+        def spread(shared, heads):
+            shape = [P, POS, len(heads), FREQS, PAIR]
+            return shared[:, :, span(heads)].unsqueeze(4).to_broadcast(shape)
+
+        def add(adder, unit, own, shared, parts=((0, 1),)):
             rotated = work.tile([P, HEADS, POS, FREQS, PAIR], F32, name="rotated")
-            count = HEADS // pieces
-            for first in range(0, HEADS, count):
-                heads = slice(first, first + count)
-                groups = slice(m * HEADS + first, m * HEADS + first + count)
+            for heads in parts:
                 adder.tensor_tensor(
-                    out=rotated[:, heads].rearrange("p h t i e -> p t h i e"),
-                    in0=shared[:, :, groups].unsqueeze(4).to_broadcast([P, POS, count, FREQS, PAIR]),
-                    in1=own[:, :, :, heads].rearrange("p e t h i -> p t h i e"),
+                    out=rotated[:, span(heads)].rearrange("p h t i e -> p t h i e"),
+                    in0=spread(shared, heads),
+                    in1=own[:, :, span(heads)],
                     op=ADD,
                 )
-                store_queue.dma_start(
-                    out=results[m][b, heads].rearrange("h (p t) d -> p h (t d)", t=POS),
-                    in_=rotated[:, heads].rearrange("p h t i e -> p h (t i e)"),
-                )
+                store(nc.sync, unit, heads, rotated)
+
+        def add_in_psum(own, shared, heads):
+            bank = banks.tile([P, POS, len(heads), FREQS, PAIR], F32, tag="bank", name="rotated_bank")
+            nc.tensor.matmul(bank[:], identity[:], own[:, :, span(heads)], start=True, stop=False)
+            nc.tensor.matmul(bank[:], identity[:], spread(shared, heads), start=False, stop=True)
+            return bank
+
+        def store_from_psum(bank, unit, heads):
+            rotated = work.tile([P, HEADS, POS, FREQS, PAIR], F32, name="rotated_copy")
+            out = rotated[:, span(heads)].rearrange("p h t i e -> p t h i e")
+            nc.scalar.copy(out=out, in_=bank[:])
+            store(nc.scalar, unit, heads, rotated)
 
         first_copies = (nc.vector.tensor_copy, nc.scalar.copy)
         for rows, grouped in (
@@ -185,35 +209,35 @@ def tile_attention_pa_s_kernel(tc, x, wq, wk, freqs_cos, freqs_sin, out_0, out_1
         quantise_x(0, 1)
         flipped = transpose(x_rows[:, 1])
         group(nc.scalar.copy, x_grouped[:, 1], flipped)
-        members = {(0, WQ): project_members(0, WQ)}
+        members, own, shared = {}, {}, {}
+        members[0, WQ] = project_members(0, WQ)
         quantise_w(WK)
         flipped = transpose(x_rows[:, 2])
         group(nc.scalar.copy, x_grouped[:, 2], flipped)
-        own = {(0, WQ): form_own(members[0, WQ])}
-        members[0, WK] = project_members(0, WK)
         flipped = transpose(x_rows[:, 3])
         group(nc.scalar.copy, x_grouped[:, 3], flipped)
+        members[0, WK] = project_members(0, WK)
         sums = project_sums(0)
+        own[0, WQ] = form_own(members[0, WQ])
         quantise_x(1, 1)
         own[0, WK] = form_own(members[0, WK])
         quantise_x(2, 1)
+        shared[0, WQ], shared[0, WK] = form_shared(sums)
         quantise_x(3, 1)
-        shared = form_shared(sums)
+        add(nc.gpsimd, (0, WQ), own[0, WQ], shared[0, WQ])
+        add(nc.gpsimd, (0, WK), own[0, WK], shared[0, WK])
 
-        late = []
-        for b in range(BATCH):
-            if b > 0:
-                members[b, WQ] = project_members(b, WQ)
-                sums = project_sums(b)
-                members[b, WK] = project_members(b, WK)
-                own[b, WQ] = form_own(members[b, WQ])
-                shared = form_shared(sums)
-                own[b, WK] = form_own(members[b, WK])
-            for m in range(MATS):
-                if MATS * b + m < GPSIMD_UNITS:
-                    add_and_store(nc.gpsimd, nc.scalar, b, m, own[b, m], shared, 1)
-                else:
-                    late.append((b, m, own[b, m], shared))
-        for b, m, own_term, shared_term in late:
-            last = (b, m) == (BATCH - 1, MATS - 1)
-            add_and_store(nc.vector, nc.sync, b, m, own_term, shared_term, 2 if last else 1)
+        for b in range(1, BATCH):
+            members[b, WQ] = project_members(b, WQ)
+            sums = project_sums(b)
+            members[b, WK] = project_members(b, WK)
+            own[b, WQ] = form_own(members[b, WQ])
+            shared[b, WQ], shared[b, WK] = form_shared(sums)
+            own[b, WK] = form_own(members[b, WK])
+        add(nc.gpsimd, (1, WQ), own[1, WQ], shared[1, WQ])
+        add(nc.gpsimd, (2, WQ), own[2, WQ], shared[2, WQ])
+        bank = add_in_psum(own[1, WK], shared[1, WK], (0, 1))
+        store_from_psum(bank, (1, WK), (0, 1))
+        add(nc.vector, (2, WK), own[2, WK], shared[2, WK])
+        add(nc.vector, (3, WQ), own[3, WQ], shared[3, WQ])
+        add(nc.vector, (3, WK), own[3, WK], shared[3, WK], ((0,), (1,)))

@@ -49,10 +49,9 @@ def tile_attention_pa_s_kernel(tc, x, wq, wk, freqs_cos, freqs_sin, out_0, out_1
             nc.sync.dma_start(out=x_rows[:, b], in_=x[b].rearrange("(p t) k -> p t k", t=POS))
 
         load_w(WQ, wq)
-        load_x(0)
-        load_w(WK, wk)
-        for b in range(1, BATCH):
+        for b in range(BATCH):
             load_x(b)
+        load_w(WK, wk)
         cos = keep.tile([P, POS, FREQS], BF16)
         sin = keep.tile([P, POS, FREQS], BF16)
         nc.scalar.dma_start(out=cos[:], in_=freqs_cos.rearrange("(p t) i -> p t i", t=POS))
@@ -127,12 +126,10 @@ def tile_attention_pa_s_kernel(tc, x, wq, wk, freqs_cos, freqs_sin, out_0, out_1
                     project(bank[:, e, t].rearrange("p h i -> p (h i)"), b, t, m, (1 - e,))
             return bank
 
-        def project_sums(b):
-            bank = banks.tile([P, POS, MATS * HEADS, FREQS], F32, tag="bank", name="sums")
+        def project_sums(b, m):
+            bank = banks.tile([P, POS, HEADS, FREQS], F32, tag="bank", name="sums")
             for t in range(POS):
-                for m in range(MATS):
-                    groups = slice(m * HEADS, (m + 1) * HEADS)
-                    project(bank[:, t, groups].rearrange("p h i -> p (h i)"), b, t, m, (EVEN, ODD))
+                project(bank[:, t].rearrange("p h i -> p (h i)"), b, t, m, (EVEN, ODD))
             return bank
 
         def form_own(bank):
@@ -146,15 +143,14 @@ def tile_attention_pa_s_kernel(tc, x, wq, wk, freqs_cos, freqs_sin, out_0, out_1
             return own
 
         def form_shared(bank):
-            groups = MATS * HEADS
-            shared = work.tile([P, POS, groups, FREQS], F32, name="shared")
+            shared = work.tile([P, POS, HEADS, FREQS], F32, name="shared")
             nc.vector.tensor_tensor(
                 out=shared[:],
                 in0=bank[:],
-                in1=cos[:].unsqueeze(2).to_broadcast([P, POS, groups, FREQS]),
+                in1=cos[:].unsqueeze(2).to_broadcast([P, POS, HEADS, FREQS]),
                 op=MULT,
             )
-            return [shared[:, :, g : g + HEADS] for g in range(0, groups, HEADS)]
+            return shared
 
         results = (out_0, out_1)
 
@@ -204,40 +200,44 @@ def tile_attention_pa_s_kernel(tc, x, wq, wk, freqs_cos, freqs_sin, out_0, out_1
                 flipped = transpose(rows[:, s : s + 1])
                 group(copy, grouped[:, s : s + 1], flipped)
         quantise_w(WQ)
-        flipped = transpose(w_rows[:, WK])
-        group(nc.scalar.copy, w_grouped[:, WK], flipped)
-        quantise_x(0, 1)
         flipped = transpose(x_rows[:, 1])
         group(nc.scalar.copy, x_grouped[:, 1], flipped)
-        members, own, shared = {}, {}, {}
-        members[0, WQ] = project_members(0, WQ)
-        quantise_w(WK)
+        quantise_x(0, 1)
         flipped = transpose(x_rows[:, 2])
         group(nc.scalar.copy, x_grouped[:, 2], flipped)
+        members0 = project_members(0, WQ)
         flipped = transpose(x_rows[:, 3])
         group(nc.scalar.copy, x_grouped[:, 3], flipped)
-        members[0, WK] = project_members(0, WK)
-        sums = project_sums(0)
-        own[0, WQ] = form_own(members[0, WQ])
-        quantise_x(1, 1)
-        own[0, WK] = form_own(members[0, WK])
-        quantise_x(2, 1)
-        shared[0, WQ], shared[0, WK] = form_shared(sums)
-        quantise_x(3, 1)
-        add(nc.gpsimd, (0, WQ), own[0, WQ], shared[0, WQ])
-        add(nc.gpsimd, (0, WK), own[0, WK], shared[0, WK])
+        flipped = transpose(w_rows[:, WK])
+        group(nc.scalar.copy, w_grouped[:, WK], flipped)
+        banks_of = {(0, WQ): (members0, project_sums(0, WQ))}
 
-        for b in range(1, BATCH):
-            members[b, WQ] = project_members(b, WQ)
-            sums = project_sums(b)
-            members[b, WK] = project_members(b, WK)
-            own[b, WQ] = form_own(members[b, WQ])
-            shared[b, WQ], shared[b, WK] = form_shared(sums)
-            own[b, WK] = form_own(members[b, WK])
-        add(nc.gpsimd, (1, WQ), own[1, WQ], shared[1, WQ])
-        add(nc.gpsimd, (2, WQ), own[2, WQ], shared[2, WQ])
-        bank = add_in_psum(own[1, WK], shared[1, WK], (0, 1))
-        store_from_psum(bank, (1, WK), (0, 1))
-        add(nc.vector, (2, WK), own[2, WK], shared[2, WK])
-        add(nc.vector, (3, WQ), own[3, WQ], shared[3, WQ])
-        add(nc.vector, (3, WK), own[3, WK], shared[3, WK], ((0,), (1,)))
+        terms = {}
+
+        def form_terms(unit):
+            members, sums = banks_of[unit]
+            own = form_own(members)
+            shared = form_shared(sums)
+            terms[unit] = (own, shared)
+
+        quantise_x(1, 1)
+        own0 = form_own(banks_of[0, WQ][0])
+        quantise_x(2, 1)
+        quantise_x(3, 1)
+        terms[0, WQ] = (own0, form_shared(banks_of[0, WQ][1]))
+        quantise_w(WK)
+        add(nc.gpsimd, (0, WQ), *terms[0, WQ])
+
+        units = [(b, m) for m in range(MATS) for b in range(BATCH)][1:]
+        for unit in units:
+            if unit == units[-1]:
+                bank = add_in_psum(*terms[2, WQ], (0,))
+                store_from_psum(bank, (2, WQ), (0,))
+            banks_of[unit] = (project_members(*unit), project_sums(*unit))
+            form_terms(unit)
+            if unit in ((1, WQ), (3, WQ), (0, WK), (1, WK)):
+                add(nc.gpsimd, unit, *terms[unit])
+        bank = add_in_psum(*terms[2, WQ], (1,))
+        store_from_psum(bank, (2, WQ), (1,))
+        add(nc.vector, (2, WK), *terms[2, WK])
+        add(nc.vector, (3, WK), *terms[3, WK], ((0,), (1,)))

@@ -26,7 +26,7 @@ MATS = 2
 WQ, WK = 0, 1
 UNITS = BATCH * MATS
 PSUM_BANKS = 8
-WARM_UP = 4
+WARM_UP = 12
 
 FLOPS = 2 * BATCH * SEQ * K * MATS * HEADS * HEAD_DIM
 
@@ -42,26 +42,38 @@ def tile_attention_pa_s_kernel(tc, x, wq, wk, freqs_cos, freqs_sin, out_0, out_1
         w_rows = keep.tile([P, MATS, PAIR, K], BF16)
         x_rows = keep.tile([P, BATCH, POS, K], BF16)
 
-        def load_w(m, w):
-            nc.sync.dma_start(out=w_rows[:, m], in_=w.rearrange("(n e) k -> n e k", e=PAIR))
+        def load(tile, matrix, parts):
+            rows = matrix.rearrange("(p s) k -> p s k", s=2)
+            for first in range(0, 2, 2 // parts):
+                part = slice(first, first + 2 // parts)
+                nc.sync.dma_start(out=tile[:, part], in_=rows[:, part])
 
-        def load_x(b):
-            nc.sync.dma_start(out=x_rows[:, b], in_=x[b].rearrange("(p t) k -> p t k", t=POS))
-
-        load_w(WQ, wq)
-        for b in range(BATCH):
-            load_x(b)
-        load_w(WK, wk)
+        load(w_rows[:, WQ], wq, 2)
+        load(x_rows[:, 0], x[0], 2)
+        for b in range(1, BATCH):
+            load(x_rows[:, b], x[b], 1)
+        load(w_rows[:, WK], wk, 1)
         cos = keep.tile([P, POS, FREQS], BF16)
         sin = keep.tile([P, POS, FREQS], BF16)
         nc.scalar.dma_start(out=cos[:], in_=freqs_cos.rearrange("(p t) i -> p t i", t=POS))
         nc.scalar.dma_start(out=sin[:], in_=freqs_sin.rearrange("(p t) i -> p t i", t=POS))
 
-        ones = keep.tile([P, P], F32)
-        nc.vector.memset(ones[:], 1.0)
-        warm = banks.tile([P, WARM_UP, P], F32, tag="bank")
+        idle = keep.tile([P, P * PACK], BF16, align_bytes=64)
+        idle_codes = keep.tile([P, P], U32, align_bytes=64)
+        idle_scales = keep.tile([P, P], U8, align_bytes=64)
+        nc.vector.memset(idle[:].bitcast(U32), 0)
+        nc.vector.quantize_mx(out=idle_codes[:].bitcast(FP8X4), scales=idle_scales[:], in_=idle[:])
+        warm = banks.tile([P, P], F32, tag="bank")
         for j in range(WARM_UP):
-            nc.tensor.matmul(warm[:, j, :], ones[:], ones[:], start=True, stop=True)
+            nc.tensor.matmul_mx(
+                out=warm[:],
+                lhsT=idle_codes[:].bitcast(FP8X4),
+                lhsT_scale=idle_scales[:],
+                rhs=idle_codes[:].bitcast(FP8X4),
+                rhs_scale=idle_scales[:],
+                start=True,
+                stop=True,
+            )
 
         identity = keep.tile([P, P], F32)
         make_identity(nc, identity[:])
@@ -99,13 +111,16 @@ def tile_attention_pa_s_kernel(tc, x, wq, wk, freqs_cos, freqs_sin, out_0, out_1
                 in_=w_grouped[:, m].rearrange("p e n j -> p (e n j)"),
             )
 
-        def quantise_x(first, count):
-            batches = slice(first, first + count)
+        def quantise_x(b, first=0, last=POS):
+            rows = slice(first * P, last * P)
             nc.vector.quantize_mx(
-                out=x_codes[:, batches].rearrange("p b c -> p (b c)").bitcast(FP8X4),
-                scales=x_scales[:, batches].rearrange("p b c -> p (b c)"),
-                in_=x_grouped[:, batches].rearrange("p b t r j -> p (b t r j)"),
+                out=x_codes[:, b, rows].bitcast(FP8X4),
+                scales=x_scales[:, b, rows],
+                in_=x_grouped[:, b, first:last].rearrange("p t r j -> p (t r j)"),
             )
+
+        def span(parts):
+            return slice(parts[0], parts[-1] + 1)
 
         def project(out, b, t, m, members):
             for e in members:
@@ -132,14 +147,17 @@ def tile_attention_pa_s_kernel(tc, x, wq, wk, freqs_cos, freqs_sin, out_0, out_1
                 project(bank[:, t].rearrange("p h i -> p (h i)"), b, t, m, (EVEN, ODD))
             return bank
 
-        def form_own(bank):
+        def form_own(bank, parts=((0, 1),)):
             own = work.tile([P, POS, HEADS, FREQS, PAIR], F32, name="own")
-            nc.vector.tensor_tensor(
-                out=own[:],
-                in0=bank[:].rearrange("p e t h i -> p t h i e"),
-                in1=own_factors[:].unsqueeze(2).to_broadcast([P, POS, HEADS, FREQS, PAIR]),
-                op=MULT,
-            )
+            for positions in parts:
+                t = span(positions)
+                factors = own_factors[:, t].unsqueeze(2)
+                nc.vector.tensor_tensor(
+                    out=own[:, t],
+                    in0=bank[:, :, t].rearrange("p e t h i -> p t h i e"),
+                    in1=factors.to_broadcast([P, len(positions), HEADS, FREQS, PAIR]),
+                    op=MULT,
+                )
             return own
 
         def form_shared(bank):
@@ -153,9 +171,6 @@ def tile_attention_pa_s_kernel(tc, x, wq, wk, freqs_cos, freqs_sin, out_0, out_1
             return shared
 
         results = (out_0, out_1)
-
-        def span(heads):
-            return slice(heads[0], heads[-1] + 1)
 
         def store(queue, unit, heads, rotated):
             b, m = unit
@@ -202,7 +217,7 @@ def tile_attention_pa_s_kernel(tc, x, wq, wk, freqs_cos, freqs_sin, out_0, out_1
         quantise_w(WQ)
         flipped = transpose(x_rows[:, 1])
         group(nc.scalar.copy, x_grouped[:, 1], flipped)
-        quantise_x(0, 1)
+        quantise_x(0)
         flipped = transpose(x_rows[:, 2])
         group(nc.scalar.copy, x_grouped[:, 2], flipped)
         members0 = project_members(0, WQ)
@@ -220,10 +235,10 @@ def tile_attention_pa_s_kernel(tc, x, wq, wk, freqs_cos, freqs_sin, out_0, out_1
             shared = form_shared(sums)
             terms[unit] = (own, shared)
 
-        quantise_x(1, 1)
-        own0 = form_own(banks_of[0, WQ][0])
-        quantise_x(2, 1)
-        quantise_x(3, 1)
+        quantise_x(1)
+        own0 = form_own(members0)
+        quantise_x(2)
+        quantise_x(3)
         terms[0, WQ] = (own0, form_shared(banks_of[0, WQ][1]))
         quantise_w(WK)
         add(nc.gpsimd, (0, WQ), *terms[0, WQ])
@@ -235,9 +250,11 @@ def tile_attention_pa_s_kernel(tc, x, wq, wk, freqs_cos, freqs_sin, out_0, out_1
                 store_from_psum(bank, (2, WQ), (0,))
             banks_of[unit] = (project_members(*unit), project_sums(*unit))
             form_terms(unit)
-            if unit in ((1, WQ), (3, WQ), (0, WK), (1, WK)):
+            if unit in ((1, WQ), (3, WQ), (0, WK)):
                 add(nc.gpsimd, unit, *terms[unit])
-        bank = add_in_psum(*terms[2, WQ], (1,))
-        store_from_psum(bank, (2, WQ), (1,))
+        for unit, head in (((2, WQ), 1), ((1, WK), 0)):
+            bank = add_in_psum(*terms[unit], (head,))
+            store_from_psum(bank, unit, (head,))
+        add(nc.vector, (1, WK), *terms[1, WK], ((1,),))
         add(nc.vector, (2, WK), *terms[2, WK])
         add(nc.vector, (3, WK), *terms[3, WK], ((0,), (1,)))

import concourse.mybir as mybir
from concourse.masks import make_identity

BF16 = mybir.dt.bfloat16
F32 = mybir.dt.float32
U32 = mybir.dt.uint32
U8 = mybir.dt.uint8
FP8X4 = mybir.dt.float8_e4m3fn_x4
MULT = mybir.AluOpType.mult
ADD = mybir.AluOpType.add
SUBTRACT = mybir.AluOpType.subtract

P = 128
BATCH = 4
SEQ = 256
K = 512
PACK = 4
HALVES = 2
HEADS = 2
HEAD_DIM = 128
FREQS = HEAD_DIM // 2
POS = SEQ // P
PAIR = 2
EVEN, ODD = 0, 1
MATS = 2
WQ, WK = 0, 1
UNITS = BATCH * MATS
PSUM_BANKS = 8
WARM_UP = 12

FLOPS = 2 * BATCH * SEQ * K * MATS * HEADS * HEAD_DIM


def tile_attention_pa_s_kernel(tc, x, wq, wk, freqs_cos, freqs_sin, out_0, out_1):
    nc = tc.nc
    with (
        tc.tile_pool(name="keep", bufs=1) as keep,
        tc.tile_pool(name="work", bufs=UNITS) as work,
        tc.psum_pool(name="banks", bufs=PSUM_BANKS) as banks,
        tc.manual_schedule(),
    ):
        w_rows = keep.tile([P, MATS, PAIR, K], BF16)
        x_rows = keep.tile([P, BATCH, POS, K], BF16)

        def load(tile, matrix, parts):
            rows = matrix.rearrange("(p s) k -> p s k", s=2)
            for first in range(0, 2, 2 // parts):
                part = slice(first, first + 2 // parts)
                nc.sync.dma_start(out=tile[:, part], in_=rows[:, part])

        load(w_rows[:, WQ], wq, 2)
        load(x_rows[:, 0], x[0], 2)
        for b in range(1, BATCH):
            load(x_rows[:, b], x[b], 1)
        load(w_rows[:, WK], wk, 1)
        cos = keep.tile([P, POS, FREQS], BF16)
        sin = keep.tile([P, POS, FREQS], BF16)
        nc.scalar.dma_start(out=cos[:], in_=freqs_cos.rearrange("(p t) i -> p t i", t=POS))
        nc.scalar.dma_start(out=sin[:], in_=freqs_sin.rearrange("(p t) i -> p t i", t=POS))

        idle = keep.tile([P, P * PACK], BF16, align_bytes=64)
        idle_codes = keep.tile([P, P], U32, align_bytes=64)
        idle_scales = keep.tile([P, P], U8, align_bytes=64)
        nc.vector.memset(idle[:].bitcast(U32), 0)
        nc.vector.quantize_mx(out=idle_codes[:].bitcast(FP8X4), scales=idle_scales[:], in_=idle[:])
        warm = banks.tile([P, P], F32, tag="bank")
        for j in range(WARM_UP):
            nc.tensor.matmul_mx(
                out=warm[:],
                lhsT=idle_codes[:].bitcast(FP8X4),
                lhsT_scale=idle_scales[:],
                rhs=idle_codes[:].bitcast(FP8X4),
                rhs_scale=idle_scales[:],
                start=True,
                stop=True,
            )

        identity = keep.tile([P, P], F32)
        make_identity(nc, identity[:])
        minus_cos = keep.tile([P, POS, FREQS], F32)
        own_factors = keep.tile([P, POS, FREQS, PAIR], F32)
        nc.gpsimd.tensor_scalar(
            out=minus_cos[:], in0=cos[:], scalar1=-1.0, scalar2=0.0, op0=MULT, op1=ADD
        )
        nc.gpsimd.tensor_tensor(out=own_factors[:, :, :, EVEN], in0=minus_cos[:], in1=sin[:], op=SUBTRACT)
        nc.gpsimd.tensor_tensor(out=own_factors[:, :, :, ODD], in0=sin[:], in1=cos[:], op=SUBTRACT)

        def transpose(rows):
            sets = rows.shape[1]
            flipped = banks.tile([P, sets, HALVES, P], F32, tag="bank")
            for s in range(sets):
                words = rows[:, s, :].bitcast(F32)
                for u in range(HALVES):
                    nc.tensor.transpose(flipped[:, s, u, :], words[:, u::HALVES], identity[:])
            return flipped

        def group(copy, grouped, flipped):
            copy(out=grouped.bitcast(F32), in_=flipped[:].rearrange("p s u r -> p s r u"))

        w_grouped = keep.tile([P, MATS, PAIR, P, PACK], BF16, align_bytes=64)
        x_grouped = keep.tile([P, BATCH, POS, P, PACK], BF16, align_bytes=64)
        w_codes = keep.tile([P, MATS, PAIR * P], U32, align_bytes=64)
        w_scales = keep.tile([P, MATS, PAIR * P], U8, align_bytes=64)
        x_codes = keep.tile([P, BATCH, POS * P], U32, align_bytes=64)
        x_scales = keep.tile([P, BATCH, POS * P], U8, align_bytes=64)

        def quantise_w(m):
            nc.vector.quantize_mx(
                out=w_codes[:, m].bitcast(FP8X4),
                scales=w_scales[:, m],
                in_=w_grouped[:, m].rearrange("p e n j -> p (e n j)"),
            )

        def quantise_x(b, first=0, last=POS):
            rows = slice(first * P, last * P)
            nc.vector.quantize_mx(
                out=x_codes[:, b, rows].bitcast(FP8X4),
                scales=x_scales[:, b, rows],
                in_=x_grouped[:, b, first:last].rearrange("p t r j -> p (t r j)"),
            )

        def span(parts):
            return slice(parts[0], parts[-1] + 1)

        def project(out, b, t, m, members):
            for e in members:
                nc.tensor.matmul_mx(
                    out=out,
                    lhsT=x_codes[:, b, t * P : (t + 1) * P].bitcast(FP8X4),
                    lhsT_scale=x_scales[:, b, t * P : (t + 1) * P],
                    rhs=w_codes[:, m, e * P : (e + 1) * P].bitcast(FP8X4),
                    rhs_scale=w_scales[:, m, e * P : (e + 1) * P],
                    start=(e == members[0]),
                    stop=(e == members[-1]),
                )

        def project_members(b, m):
            bank = banks.tile([P, PAIR, POS, HEADS, FREQS], F32, tag="bank", name="members")
            for t in range(POS):
                for e in range(PAIR):
                    project(bank[:, e, t].rearrange("p h i -> p (h i)"), b, t, m, (1 - e,))
            return bank

        def project_sums(b, m):
            bank = banks.tile([P, POS, HEADS, FREQS], F32, tag="bank", name="sums")
            for t in range(POS):
                project(bank[:, t].rearrange("p h i -> p (h i)"), b, t, m, (EVEN, ODD))
            return bank

        def form_own(bank, parts=((0, 1),)):
            own = work.tile([P, POS, HEADS, FREQS, PAIR], F32, name="own")
            for positions in parts:
                t = span(positions)
                factors = own_factors[:, t].unsqueeze(2)
                nc.vector.tensor_tensor(
                    out=own[:, t],
                    in0=bank[:, :, t].rearrange("p e t h i -> p t h i e"),
                    in1=factors.to_broadcast([P, len(positions), HEADS, FREQS, PAIR]),
                    op=MULT,
                )
            return own

        def form_shared(bank):
            shared = work.tile([P, POS, HEADS, FREQS], F32, name="shared")
            nc.vector.tensor_tensor(
                out=shared[:],
                in0=bank[:],
                in1=cos[:].unsqueeze(2).to_broadcast([P, POS, HEADS, FREQS]),
                op=MULT,
            )
            return shared

        results = (out_0, out_1)

        def store(queue, unit, heads, rotated):
            b, m = unit
            queue.dma_start(
                out=results[m][b, span(heads)].rearrange("h (p t) d -> p h (t d)", t=POS),
                in_=rotated[:, span(heads)].rearrange("p h t i e -> p h (t i e)"),
            )

        def spread(shared, heads):
            shape = [P, POS, len(heads), FREQS, PAIR]
            return shared[:, :, span(heads)].unsqueeze(4).to_broadcast(shape)

        def add(adder, unit, own, shared, parts=((0, 1),)):
            rotated = work.tile([P, HEADS, POS, FREQS, PAIR], F32, name="rotated")
            for heads in parts:
                adder.tensor_tensor(
                    out=rotated[:, span(heads)].rearrange("p h t i e -> p t h i e"),
                    in0=spread(shared, heads),
                    in1=own[:, :, span(heads)],
                    op=ADD,
                )
                store(nc.sync, unit, heads, rotated)

        def add_in_psum(own, shared, heads):
            bank = banks.tile([P, POS, len(heads), FREQS, PAIR], F32, tag="bank", name="rotated_bank")
            nc.tensor.matmul(bank[:], identity[:], own[:, :, span(heads)], start=True, stop=False)
            nc.tensor.matmul(bank[:], identity[:], spread(shared, heads), start=False, stop=True)
            return bank

        def store_from_psum(bank, unit, heads):
            rotated = work.tile([P, HEADS, POS, FREQS, PAIR], F32, name="rotated_copy")
            out = rotated[:, span(heads)].rearrange("p h t i e -> p t h i e")
            nc.scalar.copy(out=out, in_=bank[:])
            store(nc.scalar, unit, heads, rotated)

        first_copies = (nc.vector.tensor_copy, nc.scalar.copy)
        for rows, grouped in (
            (w_rows[:, WQ], w_grouped[:, WQ]),
            (x_rows[:, 0], x_grouped[:, 0]),
        ):
            for s, copy in enumerate(first_copies):
                flipped = transpose(rows[:, s : s + 1])
                group(copy, grouped[:, s : s + 1], flipped)
        quantise_w(WQ)
        flipped = transpose(x_rows[:, 1])
        group(nc.scalar.copy, x_grouped[:, 1], flipped)
        quantise_x(0)
        flipped = transpose(x_rows[:, 2])
        group(nc.scalar.copy, x_grouped[:, 2], flipped)
        members0 = project_members(0, WQ)
        flipped = transpose(x_rows[:, 3])
        group(nc.scalar.copy, x_grouped[:, 3], flipped)
        flipped = transpose(w_rows[:, WK])
        group(nc.scalar.copy, w_grouped[:, WK], flipped)
        banks_of = {(0, WQ): (members0, project_sums(0, WQ))}

        terms = {}

        def form_terms(unit):
            members, sums = banks_of[unit]
            own = form_own(members)
            shared = form_shared(sums)
            terms[unit] = (own, shared)

        quantise_x(1)
        own0 = form_own(members0)
        quantise_x(2)
        quantise_x(3)
        terms[0, WQ] = (own0, form_shared(banks_of[0, WQ][1]))
        quantise_w(WK)
        add(nc.gpsimd, (0, WQ), *terms[0, WQ])

        units = [(b, m) for m in range(MATS) for b in range(BATCH)][1:]
        for unit in units:
            if unit == units[-1]:
                bank = add_in_psum(*terms[2, WQ], (0,))
                store_from_psum(bank, (2, WQ), (0,))
            banks_of[unit] = (project_members(*unit), project_sums(*unit))
            form_terms(unit)
            if unit in ((1, WQ), (3, WQ), (0, WK)):
                add(nc.gpsimd, unit, *terms[unit])
        for unit, head in (((2, WQ), 1), ((1, WK), 0)):
            bank = add_in_psum(*terms[unit], (head,))
            store_from_psum(bank, unit, (head,))
        add(nc.vector, (1, WK), *terms[1, WK], ((1,),))
        add(nc.vector, (2, WK), *terms[2, WK])
        add(nc.vector, (3, WK), *terms[3, WK], ((0,), (1,)))
